import numpy as np
import ml_dtypes


def mxq(x, axis, fmt="e4m3"):
    dtype, down = {"e4m3": (ml_dtypes.float8_e4m3fn, 7), "e5m2": (ml_dtypes.float8_e5m2, 14)}[fmt]
    v = np.moveaxis(np.asarray(x, np.float32).astype(ml_dtypes.bfloat16).astype(np.float64), axis, -1)
    blocks = v.reshape(v.shape[:-1] + (-1, 32))
    amax = np.abs(blocks).max(-1, keepdims=True)
    byte = np.maximum(np.where(amax > 0, np.frexp(amax)[1] - 1 + 127, 0) - down, 1)
    scale = np.exp2(byte - 127.0)
    codes = (blocks / scale).astype(np.float32).astype(dtype).astype(np.float64)
    return np.moveaxis((codes * scale).reshape(v.shape), -1, axis)


WIDE = False


def mx_kscale(k):
    if not WIDE:
        return np.ones(k)
    levels = np.array([18, -18])
    if k % 512:
        return np.exp2(np.random.permutation(np.resize(levels, k // 32))).repeat(32)
    a = np.empty((k // 512, 16))
    for p in range(k // 512):
        a[p, :8] = np.random.permutation(np.resize(levels, 8))
        for g in range(8):
            far = levels[np.abs(levels - a[p, g]) >= 10]
            a[p, g + 8] = far[np.random.randint(len(far))]
    return np.exp2(a.ravel()).repeat(32)


BF16 = ml_dtypes.bfloat16


def bf(x):
    return np.asarray(x, np.float32).astype(BF16)


def f64(x):
    return np.asarray(x).astype(np.float64)


B, N, C, E = 2, 512, 1024, 1024
EPS_NORM = 1e-12


def setup_inputs():
    s = mx_kscale(N)[:, None]
    u = mx_kscale(C)
    r = mx_kscale(E)
    g = np.random.standard_normal((B, N, E)) ** 2
    cm = np.sqrt((1.0 + 0.01 * N) / 3.0)
    kv = 0.8 * np.random.standard_normal((B, E, E)) + cm * np.random.standard_normal((B, 1, E))
    q0 = bf(g / g.sum(axis=2, keepdims=True))
    kv0 = bf(kv)
    v0 = bf(np.random.standard_normal((B, N, E)))
    w0 = bf(np.random.standard_normal((E, C)) / np.sqrt(E))
    b0 = bf(0.2 * np.random.standard_normal(C))
    go = bf(6.0 * np.random.standard_normal((B, N, C)) * np.exp2(np.random.randint(-6, 1, (B, N, 1))) / s * u)
    qf = f64(q0)
    rn = 1.0 / np.maximum(np.sqrt((qf * qf).sum(axis=2, keepdims=True)), EPS_NORM)
    return {"q_feat": bf(f64(q0) * s),
            "kv": bf(f64(kv0) / r),
            "v": v0,
            "w_proj": bf(f64(w0) * r[:, None] / u),
            "b_proj": b0,
            "rnorm": np.asarray(rn, np.float32),
            "grad_out": go}


def reference(q_feat, kv, v, w_proj, b_proj, rnorm, grad_out):
    rn = f64(rnorm)
    q2 = f64(q_feat) * rn
    dh = mxq(f64(grad_out), 2, "e5m2") @ mxq(f64(w_proj), 1, "e4m3").T
    dz1 = dh / np.sqrt(N)
    dq2 = mxq(dz1, 2, "e5m2") @ np.swapaxes(mxq(f64(kv), 2, "e4m3"), 1, 2)
    dkv = np.swapaxes(mxq(q2, 1, "e4m3"), 1, 2) @ mxq(dz1, 1, "e5m2")
    dq = rn * (dq2 - q2 * (q2 * dq2).sum(axis=2, keepdims=True))
    return dq, dkv

@@ -1,0 +1,270 @@
+import math
+from contextlib import ExitStack
+
+import concourse.mybir as mybir
+from concourse.masks import make_identity
+
+B, N, C, E = 2, 512, 1024, 1024
+FLOPS = 2 * B * N * C * E + 2 * B * N * E * E + 2 * B * N * E * E
+BYTES = 2 * (B * N * E + B * E * E + E * C + B * N * C) + 4 * B * N + 4 * (B * N * E + B * E * E)
+
+F32 = mybir.dt.float32
+BF16 = mybir.dt.bfloat16
+U32 = mybir.dt.uint32
+U8 = mybir.dt.uint8
+E4M3 = mybir.dt.float8_e4m3fn_x4
+E5M2 = mybir.dt.float8_e5m2_x4
+ALU = mybir.AluOpType
+ACT = mybir.ActivationFunctionType
+
+P = 128
+BANK = 512
+RAW_BUFS = 10
+STAGE_BUFS = 7
+DZ_BUFS = 3
+DKV_BUFS = 7
+
+
+def tile_essattn_pb_v_kernel(tc, q_feat, kv, v, w_proj, b_proj, rnorm, grad_out, out_0, out_1):
+    nc = tc.nc
+    with ExitStack() as ctx:
+        keep = ctx.enter_context(tc.tile_pool(name="keep", bufs=1))
+        flow = ctx.enter_context(tc.tile_pool(name="flow", bufs=2))
+        psum = ctx.enter_context(tc.psum_pool(name="psum", bufs=1))
+        ctx.enter_context(tc.manual_schedule())
+
+        ident = keep.tile([P, P], F32, name="ident")
+        make_identity(nc, ident[:])
+
+        raw, q_sb, staged, codes, scales, dz = {}, {}, {}, {}, {}, {}
+        turn = {"s": 0, "v": 0}
+        ring = {"s": [0, 1, 2, 3, 4, 5, 6, 7], "v": [4, 5, 6, 7]}
+
+        def next_bank(reader):
+            k = ring[reader][turn[reader] % len(ring[reader])]
+            turn[reader] = turn[reader] + 1
+            return psum.tile([P, BANK], F32, name="bank%d" % k, tag="bank%d" % k)
+
+        def load_pair(key, src):
+            raw[key] = flow.tile([P, 2, C], BF16, name="raw", tag="raw", bufs=RAW_BUFS)
+            nc.sync.dma_start(out=raw[key][:], in_=src)
+
+        def load_g(b, jp):
+            load_pair(("g", b, jp), grad_out[b].rearrange("(p jp a) c -> jp p a c", jp=2, a=2)[jp])
+
+        def load_w(h, up):
+            load_pair(("w", h, up), w_proj.rearrange("(h p up a) c -> h up p a c", h=2, up=2, a=2)[h, up])
+
+        def load_k(b, i2):
+            load_pair(("k", b, i2), kv[b].rearrange("(i2 a p) c -> i2 p a c", a=2, p=P)[i2])
+
+        def load_q(b):
+            q_sb[b] = keep.tile([P, 4, E], BF16, name="q%d" % b)
+            nc.sync.dma_start(out=q_sb[b][:], in_=q_feat[b].rearrange("(p j) e -> p j e", j=4))
+
+        def stage(unit):
+            if unit not in staged:
+                staged[unit] = flow.tile([P, 4 * BANK], BF16, name="stage", tag="stage", bufs=STAGE_BUFS, align_bytes=64)
+            return staged[unit]
+
+        def copy_out(engine, out, in_):
+            if engine == "v":
+                nc.vector.tensor_copy(out=out, in_=in_)
+            else:
+                nc.scalar.copy(out=out, in_=in_)
+
+        def flip(blocks, unit, part, order, engine):
+            bank = next_bank("s")
+            for n in range(4):
+                nc.tensor.transpose(bank[:, P * n : P * (n + 1)], blocks[n], ident[:])
+            words = stage(unit)[:].bitcast(F32)[:, BANK * part : BANK * (part + 1)]
+            copy_out(
+                engine,
+                out=words.rearrange("q (%s) -> q %s" % (order, order), a=2, u=2),
+                in_=bank[:].rearrange("q (a u r) -> q %s" % order, a=2, u=2),
+            )
+
+        def input_blocks(key, g):
+            words = raw[key][:].bitcast(F32)
+            return [words[:, a, 256 * g + u : 256 * (g + 1) : 2] for a in range(2) for u in range(2)]
+
+        def flip_g(b, jp, engines="ss"):
+            for g in range(2):
+                flip(input_blocks(("g", b, jp), g), ("g", b, jp), g, "a r u", engines[g])
+
+        def flip_w(h, up, engines="ss"):
+            for g in range(2):
+                flip(input_blocks(("w", h, up), g), ("w", h, g), up, "r a u", engines[g])
+
+        def flip_k(b, i2, engines="ss"):
+            for g in range(2):
+                flip(input_blocks(("k", b, i2), g), ("k", b, i2 // 2, g), i2 % 2, "a r u", engines[g])
+
+        def flip_z(b, h, engines="ss"):
+            words = dz[b, h][:].rearrange("p t c -> p (t c)").bitcast(F32)
+            for tp in range(2):
+                blocks = [words[:, P * (4 * tp + n) : P * (4 * tp + n + 1)] for n in range(4)]
+                flip(blocks, ("z", b, h), tp, "a r u", engines[tp])
+
+        def quantize(*unit):
+            label = "_".join(str(x) for x in unit)
+            codes[unit] = keep.tile([P, BANK], U32, name="codes_" + label, align_bytes=64)
+            scales[unit] = keep.tile([P, BANK], U8, name="scales_" + label, align_bytes=64)
+            fmt = E4M3 if unit[0] in ("w", "k", "q") else E5M2
+            nc.vector.quantize_mx(out=codes[unit][:].bitcast(fmt), scales=scales[unit][:], in_=staged[unit][:])
+
+        def mx_pass(bank, still, col, moving, start, stop):
+            cols = slice(P * col, P * (col + 1))
+            nc.tensor.matmul_mx(
+                out=bank[:],
+                lhsT=codes[still][:, cols].bitcast(E4M3 if still[0] == "q" else E5M2),
+                lhsT_scale=scales[still][:, cols],
+                rhs=codes[moving][:].bitcast(E5M2 if still[0] == "q" else E4M3),
+                rhs_scale=scales[moving][:],
+                start=start,
+                stop=stop,
+            )
+
+        def dh(b, h, jp):
+            if jp == 0:
+                dz[b, h] = flow.tile([P, 4, BANK], BF16, name="dz", tag="dz", bufs=DZ_BUFS)
+            for a in range(2):
+                bank = next_bank("s")
+                for g in range(2):
+                    mx_pass(bank, ("g", b, jp), 2 * g + a, ("w", h, g), g == 0, g == 1)
+                nc.scalar.activation(out=dz[b, h][:, 2 * jp + a, :], in_=bank[:], func=ACT.Copy, scale=1.0 / math.sqrt(N))
+
+        def interleave(unit, src):
+            nc.vector.tensor_copy(
+                out=stage(unit)[:].rearrange("p (c i t) -> p c t i", i=4, t=4),
+                in_=src.rearrange("p t (c i) -> p c t i", i=4),
+            )
+
+        def weave_z(b, h):
+            interleave(("h", b, h), dz[b, h][:])
+
+        q2 = {}
+
+        def scale_q(b):
+            q2[b] = flow.tile([P, 4, E], BF16, name="q2", tag="q2", bufs=1)
+            for j in range(4):
+                nc.vector.tensor_scalar(
+                    out=q2[b][:, j, :], in0=q_sb[b][:, j, :], scalar1=rn[:, b, j : j + 1], scalar2=None, op0=ALU.mult
+                )
+
+        def weave_q(b, half):
+            interleave(("q", b, half), q2[b][:, :, BANK * half : BANK * (half + 1)])
+
+        def dkv(b, i, engines="ss"):
+            res = flow.tile([P, 2, BANK], F32, name="dkv", tag="dkv", bufs=DKV_BUFS)
+            for h in range(2):
+                bank = next_bank("s")
+                mx_pass(bank, ("q", b, i // 4), i % 4, ("h", b, h), True, True)
+                copy_out(
+                    engines[h],
+                    out=res[:, h, :].rearrange("p (r u a) -> p r u a", u=2, a=2),
+                    in_=bank[:].rearrange("p (u r a) -> p r u a", u=2, a=2),
+                )
+            nc.sync.dma_start(out=out_1[b, P * i : P * (i + 1), :], in_=res[:].rearrange("p h c -> p (h c)"))
+
+        dq_banks, sums, unscaled, results = {}, {}, {}, {}
+
+        def dq(b, t):
+            dq_banks[b, t] = [next_bank("v"), next_bank("v")]
+            for hh in range(2):
+                for g in range(2):
+                    mx_pass(dq_banks[b, t][hh], ("z", b, g), t, ("k", b, hh, g), g == 0, g == 1)
+
+        def row_sums(b, t):
+            sums[b, t] = flow.tile([P, 4], F32, name="sums", tag="sums", bufs=2)
+            for hh in range(2):
+                junk = flow.tile([P, BANK], F32, name="junk", tag="junk", bufs=2)
+                nc.vector.scalar_tensor_tensor(
+                    out=junk[:], in0=dq_banks[b, t][hh][:], scalar=neg_rn2[:, b, t : t + 1],
+                    in1=q_sb[b][:, t, BANK * hh : BANK * (hh + 1)], op0=ALU.mult, op1=ALU.mult,
+                    accum_out=sums[b, t][:, hh : hh + 1],
+                )
+
+        def join_sums(b, t):
+            nc.vector.tensor_tensor(out=sums[b, t][:, 2:3], in0=sums[b, t][:, 0:1], in1=sums[b, t][:, 1:2], op=ALU.add)
+
+        def project(b, t):
+            unscaled[b, t] = flow.tile([P, E], F32, name="unscaled", tag="unscaled", bufs=3)
+            for hh in range(2):
+                cols = slice(BANK * hh, BANK * (hh + 1))
+                nc.vector.scalar_tensor_tensor(
+                    out=unscaled[b, t][:, cols], in0=q_sb[b][:, t, cols], scalar=sums[b, t][:, 2:3],
+                    in1=dq_banks[b, t][hh][:], op0=ALU.mult, op1=ALU.add,
+                )
+
+        def finish(b, t):
+            res = flow.tile([P, E], F32, name="dq_out", tag="dq_out", bufs=4)
+            nc.vector.tensor_scalar(out=res[:], in0=unscaled[b, t][:], scalar1=rn[:, b, t : t + 1], scalar2=None, op0=ALU.mult)
+            nc.sync.dma_start(out=out_0[b].rearrange("(p j) e -> j p e", j=4)[t], in_=res[:])
+
+        def dq_scaled(b, t):
+            unscaled[b, t] = flow.tile([P, E], F32, name="unscaled", tag="unscaled", bufs=3)
+            for hh in range(2):
+                bank = next_bank("s")
+                for g in range(2):
+                    mx_pass(bank, ("z", b, g), t, ("k", b, hh, g), g == 0, g == 1)
+                nc.scalar.activation(
+                    out=unscaled[b, t][:, BANK * hh : BANK * (hh + 1)], in_=bank[:], func=ACT.Copy, scale=rn[:, b, t : t + 1]
+                )
+
+        def row_sum_scaled(b, t):
+            sums[b, t] = flow.tile([P, 4], F32, name="sums", tag="sums", bufs=2)
+            results[b, t] = flow.tile([P, E], F32, name="dq_out", tag="dq_out", bufs=4)
+            nc.vector.scalar_tensor_tensor(
+                out=results[b, t][:], in0=unscaled[b, t][:], scalar=neg_rn2[:, b, t : t + 1], in1=q_sb[b][:, t, :],
+                op0=ALU.mult, op1=ALU.mult, accum_out=sums[b, t][:, 2:3],
+            )
+
+        def project_scaled(b, t):
+            res = results[b, t]
+            nc.vector.scalar_tensor_tensor(
+                out=res[:], in0=q_sb[b][:, t, :], scalar=sums[b, t][:, 2:3], in1=unscaled[b, t][:], op0=ALU.mult, op1=ALU.add
+            )
+            nc.sync.dma_start(out=out_0[b].rearrange("(p j) e -> j p e", j=4)[t], in_=res[:])
+
+        rn = keep.tile([P, B, 4], F32, name="rn")
+        neg_rn2 = keep.tile([P, B, 4], F32, name="neg_rn2")
+
+        def load_rn():
+            nc.sync.dma_start(out=rn[:], in_=rnorm.rearrange("b (p j) o -> p b (j o)", j=4))
+
+        def square_rn():
+            nc.vector.scalar_tensor_tensor(out=neg_rn2[:], in0=rn[:], scalar=-1.0, in1=rn[:], op0=ALU.mult, op1=ALU.mult)
+
+        load_g(0, 0); load_w(0, 0); load_w(0, 1); load_g(0, 1); load_rn(); load_q(0); load_w(1, 0); load_w(1, 1)
+        load_k(0, 0); load_k(0, 1); load_k(0, 2); load_k(0, 3); load_q(1)
+        flip_g(0, 0); quantize("g", 0, 0)
+        flip_w(0, 0); flip_w(0, 1); quantize("w", 0, 0); quantize("w", 0, 1)
+        flip_g(0, 1); quantize("g", 0, 1)
+        load_g(1, 0); load_g(1, 1); load_k(1, 0); load_k(1, 1)
+        scale_q(0); weave_q(0, 0)
+        dh(0, 0, 0); dh(0, 0, 1)
+        flip_w(1, 0); flip_w(1, 1); weave_q(0, 1); quantize("w", 1, 0); quantize("w", 1, 1)
+        load_k(1, 2); load_k(1, 3)
+        weave_z(0, 0); quantize("q", 0, 0); quantize("q", 0, 1); quantize("h", 0, 0)
+        flip_k(0, 0); flip_k(0, 1)
+        dh(0, 1, 0); dh(0, 1, 1)
+        quantize("k", 0, 0, 0); quantize("k", 0, 0, 1); scale_q(1)
+        flip_z(0, 0); flip_z(0, 1); weave_z(0, 1); quantize("z", 0, 0); quantize("h", 0, 1); quantize("z", 0, 1)
+        flip_k(0, 2); flip_k(0, 3); weave_q(1, 0); square_rn(); quantize("k", 0, 1, 0); quantize("k", 0, 1, 1)
+        dkv(0, 0); dkv(0, 1)
+        flip_g(1, 0); flip_g(1, 1); weave_q(1, 1); quantize("g", 1, 0); quantize("g", 1, 1)
+        dkv(0, 2); dq_scaled(0, 0); dkv(0, 3, "vv"); quantize("q", 1, 0); row_sum_scaled(0, 0)
+        dh(1, 0, 0); dh(1, 0, 1); quantize("q", 1, 1); project_scaled(0, 0)
+        dkv(0, 4); dq_scaled(0, 1); dkv(0, 5, "vv"); weave_z(1, 0); row_sum_scaled(0, 1); quantize("h", 1, 0)
+        dh(1, 1, 0); dh(1, 1, 1); project_scaled(0, 1)
+        dkv(0, 6); dq_scaled(0, 2); weave_z(1, 1); row_sum_scaled(0, 2); quantize("h", 1, 1)
+        flip_z(1, 0); flip_z(1, 1); project_scaled(0, 2); quantize("z", 1, 0); quantize("z", 1, 1)
+        dkv(0, 7); dq_scaled(0, 3); dkv(1, 0, "vv")
+        flip_k(1, 0); flip_k(1, 1); row_sum_scaled(0, 3); quantize("k", 1, 0, 0); project_scaled(0, 3); quantize("k", 1, 0, 1)
+        flip_k(1, 2); flip_k(1, 3); quantize("k", 1, 1, 0);  quantize("k", 1, 1, 1)
+        dkv(1, 1); dkv(1, 2, "vv"); dkv(1, 3, "sv")
+        dq_scaled(1, 0); dq_scaled(1, 1)
+        row_sum_scaled(1, 0); dkv(1, 4); row_sum_scaled(1, 1); project_scaled(1, 0)
+        dq_scaled(1, 2); dkv(1, 5); project_scaled(1, 1); dq_scaled(1, 3); row_sum_scaled(1, 2)
+        dkv(1, 6); row_sum_scaled(1, 3); dkv(1, 7); project_scaled(1, 2); project_scaled(1, 3)

@@ -21,7 +21,7 @@ P = 128
 BANK = 512
 RAW_BUFS = 10
 STAGE_BUFS = 7
-DZ_BUFS = 3
+DZ_BUFS = 4
 DKV_BUFS = 7
 
 
@@ -227,6 +227,14 @@ def tile_essattn_pb_v_kernel(tc, q_feat, kv, v, w_proj, b_proj, rnorm, grad_out,
             )
             nc.sync.dma_start(out=out_0[b].rearrange("(p j) e -> j p e", j=4)[t], in_=res[:])
 
+        zeros = keep.tile([P, BANK], BF16, name="zeros")
+        nc.vector.memset(zeros[:], 0.0)
+
+        def warm(count):
+            bank = next_bank("s")
+            for n in range(count):
+                nc.tensor.matmul(bank[:], lhsT=zeros[:, 0:P], rhs=zeros[:], start=True, stop=True)
+
         rn = keep.tile([P, B, 4], F32, name="rn")
         neg_rn2 = keep.tile([P, B, 4], F32, name="neg_rn2")
 
@@ -237,34 +245,34 @@ def tile_essattn_pb_v_kernel(tc, q_feat, kv, v, w_proj, b_proj, rnorm, grad_out,
             nc.vector.scalar_tensor_tensor(out=neg_rn2[:], in0=rn[:], scalar=-1.0, in1=rn[:], op0=ALU.mult, op1=ALU.mult)
 
         load_g(0, 0); load_w(0, 0); load_w(0, 1); load_g(0, 1); load_rn(); load_q(0); load_w(1, 0); load_w(1, 1)
-        load_k(0, 0); load_k(0, 1); load_k(0, 2); load_k(0, 3); load_q(1)
+        load_g(1, 0); load_g(1, 1); load_k(0, 0); load_k(0, 1); load_q(1)
+        warm(6)
         flip_g(0, 0); quantize("g", 0, 0)
-        flip_w(0, 0); flip_w(0, 1); quantize("w", 0, 0); quantize("w", 0, 1)
-        flip_g(0, 1); quantize("g", 0, 1)
-        load_g(1, 0); load_g(1, 1); load_k(1, 0); load_k(1, 1)
-        scale_q(0); weave_q(0, 0)
-        dh(0, 0, 0); dh(0, 0, 1)
+        flip_w(0, 0); warm(1); flip_w(0, 1); quantize("w", 0, 0); quantize("w", 0, 1)
+        flip_g(0, 1); scale_q(0); quantize("g", 0, 1)
+        load_k(0, 2); load_k(0, 3); load_k(1, 0); load_k(1, 1)
+        weave_q(0, 0)
+        warm(2)
+        dh(0, 0, 0)
         flip_w(1, 0); flip_w(1, 1); weave_q(0, 1); quantize("w", 1, 0); quantize("w", 1, 1)
         load_k(1, 2); load_k(1, 3)
-        weave_z(0, 0); quantize("q", 0, 0); quantize("q", 0, 1); quantize("h", 0, 0)
-        flip_k(0, 0); flip_k(0, 1)
-        dh(0, 1, 0); dh(0, 1, 1)
-        quantize("k", 0, 0, 0); quantize("k", 0, 0, 1); scale_q(1)
-        flip_z(0, 0); flip_z(0, 1); weave_z(0, 1); quantize("z", 0, 0); quantize("h", 0, 1); quantize("z", 0, 1)
-        flip_k(0, 2); flip_k(0, 3); weave_q(1, 0); square_rn(); quantize("k", 0, 1, 0); quantize("k", 0, 1, 1)
-        dkv(0, 0); dkv(0, 1)
-        flip_g(1, 0); flip_g(1, 1); weave_q(1, 1); quantize("g", 1, 0); quantize("g", 1, 1)
-        dkv(0, 2); dq_scaled(0, 0); dkv(0, 3, "vv"); quantize("q", 1, 0); row_sum_scaled(0, 0)
-        dh(1, 0, 0); dh(1, 0, 1); quantize("q", 1, 1); project_scaled(0, 0)
-        dkv(0, 4); dq_scaled(0, 1); dkv(0, 5, "vv"); weave_z(1, 0); row_sum_scaled(0, 1); quantize("h", 1, 0)
-        dh(1, 1, 0); dh(1, 1, 1); project_scaled(0, 1)
-        dkv(0, 6); dq_scaled(0, 2); weave_z(1, 1); row_sum_scaled(0, 2); quantize("h", 1, 1)
-        flip_z(1, 0); flip_z(1, 1); project_scaled(0, 2); quantize("z", 1, 0); quantize("z", 1, 1)
-        dkv(0, 7); dq_scaled(0, 3); dkv(1, 0, "vv")
-        flip_k(1, 0); flip_k(1, 1); row_sum_scaled(0, 3); quantize("k", 1, 0, 0); project_scaled(0, 3); quantize("k", 1, 0, 1)
-        flip_k(1, 2); flip_k(1, 3); quantize("k", 1, 1, 0);  quantize("k", 1, 1, 1)
-        dkv(1, 1); dkv(1, 2, "vv"); dkv(1, 3, "sv")
+        dh(0, 0, 1)
+        flip_g(1, 0); flip_g(1, 1); quantize("q", 0, 0); quantize("q", 0, 1); weave_z(0, 0); quantize("g", 1, 0); quantize("g", 1, 1)
+        dh(0, 1, 0); dh(0, 1, 1); quantize("h", 0, 0); scale_q(1)
+        flip_k(0, 0); flip_k(0, 1); weave_z(0, 1); quantize("k", 0, 0, 0); quantize("h", 0, 1); quantize("k", 0, 0, 1)
+        dh(1, 0, 0); dh(1, 0, 1); weave_q(1, 0); square_rn()
+        flip_z(0, 0); flip_z(0, 1); dkv(0, 0); dkv(0, 1); weave_q(1, 1); quantize("z", 0, 0); quantize("q", 1, 0); quantize("z", 0, 1); weave_z(1, 0)
+        dkv(0, 2, "vv")
+        flip_k(0, 2); flip_k(0, 3); quantize("q", 1, 1); quantize("k", 0, 1, 0); quantize("k", 0, 1, 1)
+        dh(1, 1, 0); dkv(0, 3, "vv"); dh(1, 1, 1); dq_scaled(0, 0); quantize("h", 1, 0); dkv(0, 4, "vv"); dq_scaled(0, 1)
+        row_sum_scaled(0, 0); weave_z(1, 1); project_scaled(0, 0)
+        flip_z(1, 0); flip_z(1, 1); dkv(0, 5); row_sum_scaled(0, 1); quantize("h", 1, 1); dkv(0, 6); project_scaled(0, 1)
+        dq_scaled(0, 2); quantize("z", 1, 0); quantize("z", 1, 1); row_sum_scaled(0, 2)
+        flip_k(1, 0); flip_k(1, 1); dkv(0, 7, "vv"); dq_scaled(0, 3); project_scaled(0, 2)
+        quantize("k", 1, 0, 0); quantize("k", 1, 0, 1)
+        flip_k(1, 2); flip_k(1, 3); row_sum_scaled(0, 3); dkv(1, 0); quantize("k", 1, 1, 0); quantize("k", 1, 1, 1)
+        dkv(1, 1); project_scaled(0, 3); dkv(1, 2, "vv")
         dq_scaled(1, 0); dq_scaled(1, 1)
-        row_sum_scaled(1, 0); dkv(1, 4); row_sum_scaled(1, 1); project_scaled(1, 0)
-        dq_scaled(1, 2); dkv(1, 5); project_scaled(1, 1); dq_scaled(1, 3); row_sum_scaled(1, 2)
-        dkv(1, 6); row_sum_scaled(1, 3); dkv(1, 7); project_scaled(1, 2); project_scaled(1, 3)
+        row_sum_scaled(1, 0); dkv(1, 3); row_sum_scaled(1, 1); project_scaled(1, 0)
+        dq_scaled(1, 2); dkv(1, 4); project_scaled(1, 1); dq_scaled(1, 3); row_sum_scaled(1, 2)
+        dkv(1, 5); row_sum_scaled(1, 3); dkv(1, 6); dkv(1, 7); project_scaled(1, 2); project_scaled(1, 3)

@@ -19,10 +19,17 @@ ACT = mybir.ActivationFunctionType
 
 P = 128
 BANK = 512
+PSUM_BANKS = 8
+
 RAW_BUFS = 10
 STAGE_BUFS = 7
 DZ_BUFS = 4
 DKV_BUFS = 7
+SCALED_BUFS = 3
+DQ_OUT_BUFS = 4
+
+AS_FILLED = (0, 1)
+LAST_FIRST = (1, 0)
 
 
 def tile_essattn_pb_v_kernel(tc, q_feat, kv, v, w_proj, b_proj, rnorm, grad_out, out_0, out_1):
@@ -35,28 +42,31 @@ def tile_essattn_pb_v_kernel(tc, q_feat, kv, v, w_proj, b_proj, rnorm, grad_out,
 
         ident = keep.tile([P, P], F32, name="ident")
         make_identity(nc, ident[:])
+        rn = keep.tile([P, B, 4], F32, name="rn")
+        neg_rn2 = keep.tile([P, B, 4], F32, name="neg_rn2")
 
-        raw, q_sb, staged, codes, scales, dz = {}, {}, {}, {}, {}, {}
-        turn = {"s": 0, "v": 0}
-        ring = {"s": [0, 1, 2, 3, 4, 5, 6, 7], "v": [4, 5, 6, 7]}
+        raw, q_sb, q2, staged, codes, scales, dz, scaled, coef, dq_out = {}, {}, {}, {}, {}, {}, {}, {}, {}, {}
+        bank_order = list(range(PSUM_BANKS))
 
-        def next_bank(reader):
-            k = ring[reader][turn[reader] % len(ring[reader])]
-            turn[reader] = turn[reader] + 1
-            return psum.tile([P, BANK], F32, name="bank%d" % k, tag="bank%d" % k)
+        def bank_pair():
+            pair = bank_order[0:2]
+            bank_order.extend(pair)
+            bank_order.remove(pair[0])
+            bank_order.remove(pair[1])
+            return [psum.tile([P, BANK], F32, name="bank%d" % k, tag="bank%d" % k) for k in pair]
 
-        def load_pair(key, src):
+        def load_rows(key, src):
             raw[key] = flow.tile([P, 2, C], BF16, name="raw", tag="raw", bufs=RAW_BUFS)
             nc.sync.dma_start(out=raw[key][:], in_=src)
 
         def load_g(b, jp):
-            load_pair(("g", b, jp), grad_out[b].rearrange("(p jp a) c -> jp p a c", jp=2, a=2)[jp])
+            load_rows(("g", b, jp), grad_out[b].rearrange("(p jp a) c -> jp p a c", jp=2, a=2)[jp])
 
-        def load_w(h, up):
-            load_pair(("w", h, up), w_proj.rearrange("(h p up a) c -> h up p a c", h=2, up=2, a=2)[h, up])
+        def load_w(h, u):
+            load_rows(("w", h, u), w_proj.rearrange("(h p u a) c -> h u p a c", h=2, u=2, a=2)[h, u])
 
-        def load_k(b, i2):
-            load_pair(("k", b, i2), kv[b].rearrange("(i2 a p) c -> i2 p a c", a=2, p=P)[i2])
+        def load_k(b, i):
+            load_rows(("k", b, i), kv[b].rearrange("(i a p) c -> i p a c", a=2, p=P)[i])
 
         def load_q(b):
             q_sb[b] = keep.tile([P, 4, E], BF16, name="q%d" % b)
@@ -67,83 +77,44 @@ def tile_essattn_pb_v_kernel(tc, q_feat, kv, v, w_proj, b_proj, rnorm, grad_out,
                 staged[unit] = flow.tile([P, 4 * BANK], BF16, name="stage", tag="stage", bufs=STAGE_BUFS, align_bytes=64)
             return staged[unit]
 
-        def copy_out(engine, out, in_):
-            if engine == "v":
-                nc.vector.tensor_copy(out=out, in_=in_)
-            else:
-                nc.scalar.copy(out=out, in_=in_)
+        def flip(blocks, units, parts, layout, drain):
+            banks = bank_pair()
+            for n in range(2):
+                for m in range(4):
+                    nc.tensor.transpose(banks[n][:, P * m : P * (m + 1)], blocks[n][m], ident[:])
+            for n in drain:
+                pairs = stage(units[n])[:].bitcast(F32)[:, BANK * parts[n] : BANK * (parts[n] + 1)]
+                nc.scalar.copy(
+                    out=pairs.rearrange("p (%s) -> p %s" % (layout, layout), a=2, u=2),
+                    in_=banks[n][:].rearrange("p (a u r) -> p %s" % layout, a=2, u=2),
+                )
 
-        def flip(blocks, unit, part, order, engine):
-            bank = next_bank("s")
-            for n in range(4):
-                nc.tensor.transpose(bank[:, P * n : P * (n + 1)], blocks[n], ident[:])
-            words = stage(unit)[:].bitcast(F32)[:, BANK * part : BANK * (part + 1)]
-            copy_out(
-                engine,
-                out=words.rearrange("q (%s) -> q %s" % (order, order), a=2, u=2),
-                in_=bank[:].rearrange("q (a u r) -> q %s" % order, a=2, u=2),
-            )
+        def raw_blocks(key):
+            pairs = raw[key][:].bitcast(F32)
+            return [[pairs[:, a, 256 * g + u : 256 * (g + 1) : 2] for a in range(2) for u in range(2)] for g in range(2)]
 
-        def input_blocks(key, g):
-            words = raw[key][:].bitcast(F32)
-            return [words[:, a, 256 * g + u : 256 * (g + 1) : 2] for a in range(2) for u in range(2)]
+        def flip_g(b, jp, drain):
+            flip(raw_blocks(("g", b, jp)), [("g", b, jp)] * 2, [0, 1], "a r u", drain)
 
-        def flip_g(b, jp, engines="ss"):
-            for g in range(2):
-                flip(input_blocks(("g", b, jp), g), ("g", b, jp), g, "a r u", engines[g])
+        def flip_w(h, u, drain):
+            flip(raw_blocks(("w", h, u)), [("w", h, 0), ("w", h, 1)], [u, u], "r a u", drain)
 
-        def flip_w(h, up, engines="ss"):
-            for g in range(2):
-                flip(input_blocks(("w", h, up), g), ("w", h, g), up, "r a u", engines[g])
+        def flip_k(b, i, drain):
+            flip(raw_blocks(("k", b, i)), [("k", b, i // 2, 0), ("k", b, i // 2, 1)], [i % 2] * 2, "a r u", drain)
 
-        def flip_k(b, i2, engines="ss"):
-            for g in range(2):
-                flip(input_blocks(("k", b, i2), g), ("k", b, i2 // 2, g), i2 % 2, "a r u", engines[g])
+        def flip_z(b, h, drain):
+            pairs = dz[b, h][:].rearrange("p j c -> p (j c)").bitcast(F32)
+            blocks = [[pairs[:, P * (4 * jp + m) : P * (4 * jp + m + 1)] for m in range(4)] for jp in range(2)]
+            flip(blocks, [("z", b, h)] * 2, [0, 1], "a r u", drain)
 
-        def flip_z(b, h, engines="ss"):
-            words = dz[b, h][:].rearrange("p t c -> p (t c)").bitcast(F32)
-            for tp in range(2):
-                blocks = [words[:, P * (4 * tp + n) : P * (4 * tp + n + 1)] for n in range(4)]
-                flip(blocks, ("z", b, h), tp, "a r u", engines[tp])
-
-        def quantize(*unit):
-            label = "_".join(str(x) for x in unit)
-            codes[unit] = keep.tile([P, BANK], U32, name="codes_" + label, align_bytes=64)
-            scales[unit] = keep.tile([P, BANK], U8, name="scales_" + label, align_bytes=64)
-            fmt = E4M3 if unit[0] in ("w", "k", "q") else E5M2
-            nc.vector.quantize_mx(out=codes[unit][:].bitcast(fmt), scales=scales[unit][:], in_=staged[unit][:])
-
-        def mx_pass(bank, still, col, moving, start, stop):
-            cols = slice(P * col, P * (col + 1))
-            nc.tensor.matmul_mx(
-                out=bank[:],
-                lhsT=codes[still][:, cols].bitcast(E4M3 if still[0] == "q" else E5M2),
-                lhsT_scale=scales[still][:, cols],
-                rhs=codes[moving][:].bitcast(E5M2 if still[0] == "q" else E4M3),
-                rhs_scale=scales[moving][:],
-                start=start,
-                stop=stop,
-            )
-
-        def dh(b, h, jp):
-            if jp == 0:
-                dz[b, h] = flow.tile([P, 4, BANK], BF16, name="dz", tag="dz", bufs=DZ_BUFS)
-            for a in range(2):
-                bank = next_bank("s")
-                for g in range(2):
-                    mx_pass(bank, ("g", b, jp), 2 * g + a, ("w", h, g), g == 0, g == 1)
-                nc.scalar.activation(out=dz[b, h][:, 2 * jp + a, :], in_=bank[:], func=ACT.Copy, scale=1.0 / math.sqrt(N))
-
-        def interleave(unit, src):
+        def weave(unit, slots):
             nc.vector.tensor_copy(
-                out=stage(unit)[:].rearrange("p (c i t) -> p c t i", i=4, t=4),
-                in_=src.rearrange("p t (c i) -> p c t i", i=4),
+                out=stage(unit)[:].rearrange("p (c i j) -> p c j i", i=4, j=4),
+                in_=slots.rearrange("p j (c i) -> p c j i", i=4),
             )
 
         def weave_z(b, h):
-            interleave(("h", b, h), dz[b, h][:])
-
-        q2 = {}
+            weave(("t", b, h), dz[b, h][:])
 
         def scale_q(b):
             q2[b] = flow.tile([P, 4, E], BF16, name="q2", tag="q2", bufs=1)
@@ -153,126 +124,216 @@ def tile_essattn_pb_v_kernel(tc, q_feat, kv, v, w_proj, b_proj, rnorm, grad_out,
                 )
 
         def weave_q(b, half):
-            interleave(("q", b, half), q2[b][:, :, BANK * half : BANK * (half + 1)])
+            weave(("q", b, half), q2[b][:, :, BANK * half : BANK * (half + 1)])
 
-        def dkv(b, i, engines="ss"):
+        def fmt(unit):
+            return E4M3 if unit[0] in ("w", "k", "q") else E5M2
+
+        def quantize(*unit):
+            label = "_".join(str(x) for x in unit)
+            codes[unit] = keep.tile([P, BANK], U32, name="codes_" + label, align_bytes=64)
+            scales[unit] = keep.tile([P, BANK], U8, name="scales_" + label, align_bytes=64)
+            nc.vector.quantize_mx(out=codes[unit][:].bitcast(fmt(unit)), scales=scales[unit][:], in_=staged[unit][:])
+
+        def mx_pass(bank, still, block, moving, start, stop):
+            cols = slice(P * block, P * (block + 1))
+            nc.tensor.matmul_mx(
+                out=bank[:],
+                lhsT=codes[still][:, cols].bitcast(fmt(still)),
+                lhsT_scale=scales[still][:, cols],
+                rhs=codes[moving][:].bitcast(fmt(moving)),
+                rhs_scale=scales[moving][:],
+                start=start,
+                stop=stop,
+            )
+
+        def dh(b, h, jp, drain):
+            if jp == 0:
+                dz[b, h] = flow.tile([P, 4, BANK], BF16, name="dz", tag="dz", bufs=DZ_BUFS)
+            banks = bank_pair()
+            for a in range(2):
+                for g in range(2):
+                    mx_pass(banks[a], ("g", b, jp), 2 * g + a, ("w", h, g), g == 0, g == 1)
+            for a in drain:
+                nc.scalar.activation(out=dz[b, h][:, 2 * jp + a, :], in_=banks[a][:], func=ACT.Copy, scale=1.0 / math.sqrt(N))
+
+        def dkv(b, i, copies=(nc.scalar.copy, nc.scalar.copy)):
             res = flow.tile([P, 2, BANK], F32, name="dkv", tag="dkv", bufs=DKV_BUFS)
+            banks = bank_pair()
             for h in range(2):
-                bank = next_bank("s")
-                mx_pass(bank, ("q", b, i // 4), i % 4, ("h", b, h), True, True)
-                copy_out(
-                    engines[h],
+                mx_pass(banks[h], ("q", b, i // 4), i % 4, ("t", b, h), True, True)
+            for h in LAST_FIRST:
+                copies[h](
                     out=res[:, h, :].rearrange("p (r u a) -> p r u a", u=2, a=2),
-                    in_=bank[:].rearrange("p (u r a) -> p r u a", u=2, a=2),
+                    in_=banks[h][:].rearrange("p (u r a) -> p r u a", u=2, a=2),
                 )
             nc.sync.dma_start(out=out_1[b, P * i : P * (i + 1), :], in_=res[:].rearrange("p h c -> p (h c)"))
 
-        dq_banks, sums, unscaled, results = {}, {}, {}, {}
-
-        def dq(b, t):
-            dq_banks[b, t] = [next_bank("v"), next_bank("v")]
-            for hh in range(2):
+        def dq(b, j):
+            scaled[b, j] = flow.tile([P, E], F32, name="scaled", tag="scaled", bufs=SCALED_BUFS)
+            banks = bank_pair()
+            for half in range(2):
                 for g in range(2):
-                    mx_pass(dq_banks[b, t][hh], ("z", b, g), t, ("k", b, hh, g), g == 0, g == 1)
-
-        def row_sums(b, t):
-            sums[b, t] = flow.tile([P, 4], F32, name="sums", tag="sums", bufs=2)
-            for hh in range(2):
-                junk = flow.tile([P, BANK], F32, name="junk", tag="junk", bufs=2)
-                nc.vector.scalar_tensor_tensor(
-                    out=junk[:], in0=dq_banks[b, t][hh][:], scalar=neg_rn2[:, b, t : t + 1],
-                    in1=q_sb[b][:, t, BANK * hh : BANK * (hh + 1)], op0=ALU.mult, op1=ALU.mult,
-                    accum_out=sums[b, t][:, hh : hh + 1],
-                )
-
-        def join_sums(b, t):
-            nc.vector.tensor_tensor(out=sums[b, t][:, 2:3], in0=sums[b, t][:, 0:1], in1=sums[b, t][:, 1:2], op=ALU.add)
-
-        def project(b, t):
-            unscaled[b, t] = flow.tile([P, E], F32, name="unscaled", tag="unscaled", bufs=3)
-            for hh in range(2):
-                cols = slice(BANK * hh, BANK * (hh + 1))
-                nc.vector.scalar_tensor_tensor(
-                    out=unscaled[b, t][:, cols], in0=q_sb[b][:, t, cols], scalar=sums[b, t][:, 2:3],
-                    in1=dq_banks[b, t][hh][:], op0=ALU.mult, op1=ALU.add,
-                )
-
-        def finish(b, t):
-            res = flow.tile([P, E], F32, name="dq_out", tag="dq_out", bufs=4)
-            nc.vector.tensor_scalar(out=res[:], in0=unscaled[b, t][:], scalar1=rn[:, b, t : t + 1], scalar2=None, op0=ALU.mult)
-            nc.sync.dma_start(out=out_0[b].rearrange("(p j) e -> j p e", j=4)[t], in_=res[:])
-
-        def dq_scaled(b, t):
-            unscaled[b, t] = flow.tile([P, E], F32, name="unscaled", tag="unscaled", bufs=3)
-            for hh in range(2):
-                bank = next_bank("s")
-                for g in range(2):
-                    mx_pass(bank, ("z", b, g), t, ("k", b, hh, g), g == 0, g == 1)
+                    mx_pass(banks[half], ("z", b, g), j, ("k", b, half, g), g == 0, g == 1)
+            for half in LAST_FIRST:
                 nc.scalar.activation(
-                    out=unscaled[b, t][:, BANK * hh : BANK * (hh + 1)], in_=bank[:], func=ACT.Copy, scale=rn[:, b, t : t + 1]
+                    out=scaled[b, j][:, BANK * half : BANK * (half + 1)], in_=banks[half][:], func=ACT.Copy, scale=rn[:, b, j : j + 1]
                 )
 
-        def row_sum_scaled(b, t):
-            sums[b, t] = flow.tile([P, 4], F32, name="sums", tag="sums", bufs=2)
-            results[b, t] = flow.tile([P, E], F32, name="dq_out", tag="dq_out", bufs=4)
+        def row_sum(b, j):
+            coef[b, j] = flow.tile([P, 1], F32, name="coef", tag="coef")
+            dq_out[b, j] = flow.tile([P, E], F32, name="dq_out", tag="dq_out", bufs=DQ_OUT_BUFS)
             nc.vector.scalar_tensor_tensor(
-                out=results[b, t][:], in0=unscaled[b, t][:], scalar=neg_rn2[:, b, t : t + 1], in1=q_sb[b][:, t, :],
-                op0=ALU.mult, op1=ALU.mult, accum_out=sums[b, t][:, 2:3],
+                out=dq_out[b, j][:],
+                in0=scaled[b, j][:],
+                scalar=neg_rn2[:, b, j : j + 1],
+                in1=q_sb[b][:, j, :],
+                op0=ALU.mult,
+                op1=ALU.mult,
+                accum_out=coef[b, j][:],
             )
 
-        def project_scaled(b, t):
-            res = results[b, t]
-            nc.vector.scalar_tensor_tensor(
-                out=res[:], in0=q_sb[b][:, t, :], scalar=sums[b, t][:, 2:3], in1=unscaled[b, t][:], op0=ALU.mult, op1=ALU.add
-            )
-            nc.sync.dma_start(out=out_0[b].rearrange("(p j) e -> j p e", j=4)[t], in_=res[:])
+        def project(b, j, pieces=1):
+            rows = out_0[b].rearrange("(p j) e -> j p e", j=4)[j]
+            for n in range(pieces):
+                cols = slice(E * n // pieces, E * (n + 1) // pieces)
+                nc.vector.scalar_tensor_tensor(
+                    out=dq_out[b, j][:, cols],
+                    in0=q_sb[b][:, j, cols],
+                    scalar=coef[b, j][:],
+                    in1=scaled[b, j][:, cols],
+                    op0=ALU.mult,
+                    op1=ALU.add,
+                )
+                nc.sync.dma_start(out=rows[:, cols], in_=dq_out[b, j][:, cols])
 
-        zeros = keep.tile([P, BANK], BF16, name="zeros")
-        nc.vector.memset(zeros[:], 0.0)
+        on_vector = (nc.vector.tensor_copy, nc.vector.tensor_copy)
+        shared = (nc.scalar.copy, nc.vector.tensor_copy)
 
-        def warm(count):
-            bank = next_bank("s")
-            for n in range(count):
-                nc.tensor.matmul(bank[:], lhsT=zeros[:, 0:P], rhs=zeros[:], start=True, stop=True)
+        nc.scalar.dma_start(out=rn[:], in_=rnorm.rearrange("b (p j) o -> p b (j o)", j=4))
+        load_g(0, 0)
+        load_w(0, 0)
+        load_w(0, 1)
+        load_g(0, 1)
+        load_q(0)
+        load_w(1, 0)
+        load_w(1, 1)
+        for i in range(4):
+            load_k(0, i)
+        load_q(1)
 
-        rn = keep.tile([P, B, 4], F32, name="rn")
-        neg_rn2 = keep.tile([P, B, 4], F32, name="neg_rn2")
-
-        def load_rn():
-            nc.sync.dma_start(out=rn[:], in_=rnorm.rearrange("b (p j) o -> p b (j o)", j=4))
-
-        def square_rn():
-            nc.vector.scalar_tensor_tensor(out=neg_rn2[:], in0=rn[:], scalar=-1.0, in1=rn[:], op0=ALU.mult, op1=ALU.mult)
-
-        load_g(0, 0); load_w(0, 0); load_w(0, 1); load_g(0, 1); load_rn(); load_q(0); load_w(1, 0); load_w(1, 1)
-        load_g(1, 0); load_g(1, 1); load_k(0, 0); load_k(0, 1); load_q(1)
-        warm(6)
-        flip_g(0, 0); quantize("g", 0, 0)
-        flip_w(0, 0); warm(1); flip_w(0, 1); quantize("w", 0, 0); quantize("w", 0, 1)
-        flip_g(0, 1); scale_q(0); quantize("g", 0, 1)
-        load_k(0, 2); load_k(0, 3); load_k(1, 0); load_k(1, 1)
+        flip_g(0, 0, AS_FILLED)
+        quantize("g", 0, 0)
+        flip_w(0, 0, AS_FILLED)
+        flip_w(0, 1, AS_FILLED)
+        quantize("w", 0, 0)
+        quantize("w", 0, 1)
+        flip_g(0, 1, AS_FILLED)
+        quantize("g", 0, 1)
+        load_g(1, 0)
+        load_g(1, 1)
+        load_k(1, 0)
+        load_k(1, 1)
+        scale_q(0)
         weave_q(0, 0)
-        warm(2)
-        dh(0, 0, 0)
-        flip_w(1, 0); flip_w(1, 1); weave_q(0, 1); quantize("w", 1, 0); quantize("w", 1, 1)
-        load_k(1, 2); load_k(1, 3)
-        dh(0, 0, 1)
-        flip_g(1, 0); flip_g(1, 1); quantize("q", 0, 0); quantize("q", 0, 1); weave_z(0, 0); quantize("g", 1, 0); quantize("g", 1, 1)
-        dh(0, 1, 0); dh(0, 1, 1); quantize("h", 0, 0); scale_q(1)
-        flip_k(0, 0); flip_k(0, 1); weave_z(0, 1); quantize("k", 0, 0, 0); quantize("h", 0, 1); quantize("k", 0, 0, 1)
-        dh(1, 0, 0); dh(1, 0, 1); weave_q(1, 0); square_rn()
-        flip_z(0, 0); flip_z(0, 1); dkv(0, 0); dkv(0, 1); weave_q(1, 1); quantize("z", 0, 0); quantize("q", 1, 0); quantize("z", 0, 1); weave_z(1, 0)
-        dkv(0, 2, "vv")
-        flip_k(0, 2); flip_k(0, 3); quantize("q", 1, 1); quantize("k", 0, 1, 0); quantize("k", 0, 1, 1)
-        dh(1, 1, 0); dkv(0, 3, "vv"); dh(1, 1, 1); dq_scaled(0, 0); quantize("h", 1, 0); dkv(0, 4, "vv"); dq_scaled(0, 1)
-        row_sum_scaled(0, 0); weave_z(1, 1); project_scaled(0, 0)
-        flip_z(1, 0); flip_z(1, 1); dkv(0, 5); row_sum_scaled(0, 1); quantize("h", 1, 1); dkv(0, 6); project_scaled(0, 1)
-        dq_scaled(0, 2); quantize("z", 1, 0); quantize("z", 1, 1); row_sum_scaled(0, 2)
-        flip_k(1, 0); flip_k(1, 1); dkv(0, 7, "vv"); dq_scaled(0, 3); project_scaled(0, 2)
-        quantize("k", 1, 0, 0); quantize("k", 1, 0, 1)
-        flip_k(1, 2); flip_k(1, 3); row_sum_scaled(0, 3); dkv(1, 0); quantize("k", 1, 1, 0); quantize("k", 1, 1, 1)
-        dkv(1, 1); project_scaled(0, 3); dkv(1, 2, "vv")
-        dq_scaled(1, 0); dq_scaled(1, 1)
-        row_sum_scaled(1, 0); dkv(1, 3); row_sum_scaled(1, 1); project_scaled(1, 0)
-        dq_scaled(1, 2); dkv(1, 4); project_scaled(1, 1); dq_scaled(1, 3); row_sum_scaled(1, 2)
-        dkv(1, 5); row_sum_scaled(1, 3); dkv(1, 6); dkv(1, 7); project_scaled(1, 2); project_scaled(1, 3)
+        dh(0, 0, 0, AS_FILLED)
+        dh(0, 0, 1, AS_FILLED)
+        flip_w(1, 0, AS_FILLED)
+        flip_w(1, 1, AS_FILLED)
+        weave_q(0, 1)
+        quantize("w", 1, 0)
+        quantize("w", 1, 1)
+        load_k(1, 2)
+        load_k(1, 3)
+        weave_z(0, 0)
+        quantize("q", 0, 0)
+        quantize("q", 0, 1)
+        quantize("t", 0, 0)
+        flip_k(0, 0, AS_FILLED)
+        flip_k(0, 1, AS_FILLED)
+        dh(0, 1, 0, AS_FILLED)
+        dh(0, 1, 1, AS_FILLED)
+        quantize("k", 0, 0, 0)
+        quantize("k", 0, 0, 1)
+        scale_q(1)
+        flip_z(0, 0, AS_FILLED)
+        flip_z(0, 1, AS_FILLED)
+        weave_z(0, 1)
+        quantize("z", 0, 0)
+        quantize("t", 0, 1)
+        quantize("z", 0, 1)
+        flip_k(0, 2, LAST_FIRST)
+        flip_k(0, 3, LAST_FIRST)
+        weave_q(1, 0)
+        nc.vector.scalar_tensor_tensor(out=neg_rn2[:], in0=rn[:], scalar=-1.0, in1=rn[:], op0=ALU.mult, op1=ALU.mult)
+        quantize("k", 0, 1, 0)
+        quantize("k", 0, 1, 1)
+
+        dkv(0, 0)
+        dkv(0, 1)
+        flip_g(1, 0, LAST_FIRST)
+        flip_g(1, 1, LAST_FIRST)
+        weave_q(1, 1)
+        quantize("g", 1, 0)
+        quantize("g", 1, 1)
+        dkv(0, 2)
+        dq(0, 0)
+        dkv(0, 3, on_vector)
+        quantize("q", 1, 0)
+        row_sum(0, 0)
+        dh(1, 0, 0, LAST_FIRST)
+        dh(1, 0, 1, LAST_FIRST)
+        quantize("q", 1, 1)
+        project(0, 0)
+        dkv(0, 4)
+        dq(0, 1)
+        dkv(0, 5, on_vector)
+        weave_z(1, 0)
+        row_sum(0, 1)
+        quantize("t", 1, 0)
+        dh(1, 1, 0, LAST_FIRST)
+        dh(1, 1, 1, LAST_FIRST)
+        project(0, 1)
+        dkv(0, 6)
+        dq(0, 2)
+        weave_z(1, 1)
+        row_sum(0, 2)
+        quantize("t", 1, 1)
+        flip_z(1, 0, LAST_FIRST)
+        flip_z(1, 1, LAST_FIRST)
+        project(0, 2)
+        quantize("z", 1, 0)
+        quantize("z", 1, 1)
+        dkv(0, 7)
+        dq(0, 3)
+        dkv(1, 0, on_vector)
+        flip_k(1, 0, LAST_FIRST)
+        flip_k(1, 1, LAST_FIRST)
+        row_sum(0, 3)
+        quantize("k", 1, 0, 0)
+        project(0, 3)
+        quantize("k", 1, 0, 1)
+        flip_k(1, 2, LAST_FIRST)
+        flip_k(1, 3, LAST_FIRST)
+        quantize("k", 1, 1, 0)
+        quantize("k", 1, 1, 1)
+
+        dkv(1, 1)
+        dkv(1, 2, on_vector)
+        dkv(1, 3, shared)
+        dq(1, 0)
+        dq(1, 1)
+        row_sum(1, 0)
+        dkv(1, 4)
+        row_sum(1, 1)
+        project(1, 0)
+        dq(1, 2)
+        dkv(1, 5)
+        project(1, 1)
+        dq(1, 3)
+        row_sum(1, 2)
+        dkv(1, 6)
+        row_sum(1, 3)
+        dkv(1, 7)
+        project(1, 2)
+        project(1, 3, pieces=2)

@@ -28,9 +28,6 @@ DKV_BUFS = 7
 SCALED_BUFS = 3
 DQ_OUT_BUFS = 4
 
-AS_FILLED = (0, 1)
-LAST_FIRST = (1, 0)
-
 
 def tile_essattn_pb_v_kernel(tc, q_feat, kv, v, w_proj, b_proj, rnorm, grad_out, out_0, out_1):
     nc = tc.nc
@@ -62,11 +59,11 @@ def tile_essattn_pb_v_kernel(tc, q_feat, kv, v, w_proj, b_proj, rnorm, grad_out,
         def load_g(b, jp):
             load_rows(("g", b, jp), grad_out[b].rearrange("(p jp a) c -> jp p a c", jp=2, a=2)[jp])
 
-        def load_w(h, u):
-            load_rows(("w", h, u), w_proj.rearrange("(h p u a) c -> h u p a c", h=2, u=2, a=2)[h, u])
+        def load_w(h, uz):
+            load_rows(("w", h, uz), w_proj.rearrange("(h p uz a) c -> h uz p a c", h=2, uz=2, a=2)[h, uz])
 
-        def load_k(b, i):
-            load_rows(("k", b, i), kv[b].rearrange("(i a p) c -> i p a c", a=2, p=P)[i])
+        def load_k(b, kt):
+            load_rows(("k", b, kt), kv[b].rearrange("(kt a p) c -> kt p a c", a=2, p=P)[kt])
 
         def load_q(b):
             q_sb[b] = keep.tile([P, 4, E], BF16, name="q%d" % b)
@@ -77,12 +74,12 @@ def tile_essattn_pb_v_kernel(tc, q_feat, kv, v, w_proj, b_proj, rnorm, grad_out,
                 staged[unit] = flow.tile([P, 4 * BANK], BF16, name="stage", tag="stage", bufs=STAGE_BUFS, align_bytes=64)
             return staged[unit]
 
-        def flip(blocks, units, parts, layout, drain):
+        def flip(blocks, units, parts, layout):
             banks = bank_pair()
             for n in range(2):
                 for m in range(4):
                     nc.tensor.transpose(banks[n][:, P * m : P * (m + 1)], blocks[n][m], ident[:])
-            for n in drain:
+            for n in range(2):
                 pairs = stage(units[n])[:].bitcast(F32)[:, BANK * parts[n] : BANK * (parts[n] + 1)]
                 nc.scalar.copy(
                     out=pairs.rearrange("p (%s) -> p %s" % (layout, layout), a=2, u=2),
@@ -93,24 +90,24 @@ def tile_essattn_pb_v_kernel(tc, q_feat, kv, v, w_proj, b_proj, rnorm, grad_out,
             pairs = raw[key][:].bitcast(F32)
             return [[pairs[:, a, 256 * g + u : 256 * (g + 1) : 2] for a in range(2) for u in range(2)] for g in range(2)]
 
-        def flip_g(b, jp, drain):
-            flip(raw_blocks(("g", b, jp)), [("g", b, jp)] * 2, [0, 1], "a r u", drain)
+        def flip_g(b, jp):
+            flip(raw_blocks(("g", b, jp)), [("g", b, jp)] * 2, [0, 1], "a r u")
 
-        def flip_w(h, u, drain):
-            flip(raw_blocks(("w", h, u)), [("w", h, 0), ("w", h, 1)], [u, u], "r a u", drain)
+        def flip_w(h, uz):
+            flip(raw_blocks(("w", h, uz)), [("w", h, 0), ("w", h, 1)], [uz, uz], "r a u")
 
-        def flip_k(b, i, drain):
-            flip(raw_blocks(("k", b, i)), [("k", b, i // 2, 0), ("k", b, i // 2, 1)], [i % 2] * 2, "a r u", drain)
+        def flip_k(b, kt):
+            flip(raw_blocks(("k", b, kt)), [("k", b, kt // 2, 0), ("k", b, kt // 2, 1)], [kt % 2] * 2, "a r u")
 
-        def flip_z(b, h, drain):
+        def flip_z(b, h):
             pairs = dz[b, h][:].rearrange("p j c -> p (j c)").bitcast(F32)
             blocks = [[pairs[:, P * (4 * jp + m) : P * (4 * jp + m + 1)] for m in range(4)] for jp in range(2)]
-            flip(blocks, [("z", b, h)] * 2, [0, 1], "a r u", drain)
+            flip(blocks, [("z", b, h)] * 2, [0, 1], "a r u")
 
         def weave(unit, slots):
             nc.vector.tensor_copy(
-                out=stage(unit)[:].rearrange("p (c i j) -> p c j i", i=4, j=4),
-                in_=slots.rearrange("p j (c i) -> p c j i", i=4),
+                out=stage(unit)[:].rearrange("p (c x j) -> p c j x", x=4, j=4),
+                in_=slots.rearrange("p j (c x) -> p c j x", x=4),
             )
 
         def weave_z(b, h):
@@ -147,14 +144,14 @@ def tile_essattn_pb_v_kernel(tc, q_feat, kv, v, w_proj, b_proj, rnorm, grad_out,
                 stop=stop,
             )
 
-        def dh(b, h, jp, drain):
+        def dh(b, h, jp):
             if jp == 0:
                 dz[b, h] = flow.tile([P, 4, BANK], BF16, name="dz", tag="dz", bufs=DZ_BUFS)
             banks = bank_pair()
             for a in range(2):
                 for g in range(2):
                     mx_pass(banks[a], ("g", b, jp), 2 * g + a, ("w", h, g), g == 0, g == 1)
-            for a in drain:
+            for a in range(2):
                 nc.scalar.activation(out=dz[b, h][:, 2 * jp + a, :], in_=banks[a][:], func=ACT.Copy, scale=1.0 / math.sqrt(N))
 
         def dkv(b, i, copies=(nc.scalar.copy, nc.scalar.copy)):
@@ -162,10 +159,10 @@ def tile_essattn_pb_v_kernel(tc, q_feat, kv, v, w_proj, b_proj, rnorm, grad_out,
             banks = bank_pair()
             for h in range(2):
                 mx_pass(banks[h], ("q", b, i // 4), i % 4, ("t", b, h), True, True)
-            for h in LAST_FIRST:
+            for h in range(2):
                 copies[h](
-                    out=res[:, h, :].rearrange("p (r u a) -> p r u a", u=2, a=2),
-                    in_=banks[h][:].rearrange("p (u r a) -> p r u a", u=2, a=2),
+                    out=res[:, h, :].rearrange("p (r uz a) -> p r uz a", uz=2, a=2),
+                    in_=banks[h][:].rearrange("p (uz r a) -> p r uz a", uz=2, a=2),
                 )
             nc.sync.dma_start(out=out_1[b, P * i : P * (i + 1), :], in_=res[:].rearrange("p h c -> p (h c)"))
 
@@ -175,7 +172,7 @@ def tile_essattn_pb_v_kernel(tc, q_feat, kv, v, w_proj, b_proj, rnorm, grad_out,
             for half in range(2):
                 for g in range(2):
                     mx_pass(banks[half], ("z", b, g), j, ("k", b, half, g), g == 0, g == 1)
-            for half in LAST_FIRST:
+            for half in range(2):
                 nc.scalar.activation(
                     out=scaled[b, j][:, BANK * half : BANK * (half + 1)], in_=banks[half][:], func=ACT.Copy, scale=rn[:, b, j : j + 1]
                 )
@@ -218,17 +215,17 @@ def tile_essattn_pb_v_kernel(tc, q_feat, kv, v, w_proj, b_proj, rnorm, grad_out,
         load_q(0)
         load_w(1, 0)
         load_w(1, 1)
-        for i in range(4):
-            load_k(0, i)
+        for kt in range(4):
+            load_k(0, kt)
         load_q(1)
 
-        flip_g(0, 0, AS_FILLED)
+        flip_g(0, 0)
         quantize("g", 0, 0)
-        flip_w(0, 0, AS_FILLED)
-        flip_w(0, 1, AS_FILLED)
+        flip_w(0, 0)
+        flip_w(0, 1)
         quantize("w", 0, 0)
         quantize("w", 0, 1)
-        flip_g(0, 1, AS_FILLED)
+        flip_g(0, 1)
         quantize("g", 0, 1)
         load_g(1, 0)
         load_g(1, 1)
@@ -236,10 +233,10 @@ def tile_essattn_pb_v_kernel(tc, q_feat, kv, v, w_proj, b_proj, rnorm, grad_out,
         load_k(1, 1)
         scale_q(0)
         weave_q(0, 0)
-        dh(0, 0, 0, AS_FILLED)
-        dh(0, 0, 1, AS_FILLED)
-        flip_w(1, 0, AS_FILLED)
-        flip_w(1, 1, AS_FILLED)
+        dh(0, 0, 0)
+        dh(0, 0, 1)
+        flip_w(1, 0)
+        flip_w(1, 1)
         weave_q(0, 1)
         quantize("w", 1, 0)
         quantize("w", 1, 1)
@@ -249,21 +246,21 @@ def tile_essattn_pb_v_kernel(tc, q_feat, kv, v, w_proj, b_proj, rnorm, grad_out,
         quantize("q", 0, 0)
         quantize("q", 0, 1)
         quantize("t", 0, 0)
-        flip_k(0, 0, AS_FILLED)
-        flip_k(0, 1, AS_FILLED)
-        dh(0, 1, 0, AS_FILLED)
-        dh(0, 1, 1, AS_FILLED)
+        flip_k(0, 0)
+        flip_k(0, 1)
+        dh(0, 1, 0)
+        dh(0, 1, 1)
         quantize("k", 0, 0, 0)
         quantize("k", 0, 0, 1)
         scale_q(1)
-        flip_z(0, 0, AS_FILLED)
-        flip_z(0, 1, AS_FILLED)
+        flip_z(0, 0)
+        flip_z(0, 1)
         weave_z(0, 1)
         quantize("z", 0, 0)
         quantize("t", 0, 1)
         quantize("z", 0, 1)
-        flip_k(0, 2, LAST_FIRST)
-        flip_k(0, 3, LAST_FIRST)
+        flip_k(0, 2)
+        flip_k(0, 3)
         weave_q(1, 0)
         nc.vector.scalar_tensor_tensor(out=neg_rn2[:], in0=rn[:], scalar=-1.0, in1=rn[:], op0=ALU.mult, op1=ALU.mult)
         quantize("k", 0, 1, 0)
@@ -271,8 +268,8 @@ def tile_essattn_pb_v_kernel(tc, q_feat, kv, v, w_proj, b_proj, rnorm, grad_out,
 
         dkv(0, 0)
         dkv(0, 1)
-        flip_g(1, 0, LAST_FIRST)
-        flip_g(1, 1, LAST_FIRST)
+        flip_g(1, 0)
+        flip_g(1, 1)
         weave_q(1, 1)
         quantize("g", 1, 0)
         quantize("g", 1, 1)
@@ -281,8 +278,8 @@ def tile_essattn_pb_v_kernel(tc, q_feat, kv, v, w_proj, b_proj, rnorm, grad_out,
         dkv(0, 3, on_vector)
         quantize("q", 1, 0)
         row_sum(0, 0)
-        dh(1, 0, 0, LAST_FIRST)
-        dh(1, 0, 1, LAST_FIRST)
+        dh(1, 0, 0)
+        dh(1, 0, 1)
         quantize("q", 1, 1)
         project(0, 0)
         dkv(0, 4)
@@ -291,30 +288,30 @@ def tile_essattn_pb_v_kernel(tc, q_feat, kv, v, w_proj, b_proj, rnorm, grad_out,
         weave_z(1, 0)
         row_sum(0, 1)
         quantize("t", 1, 0)
-        dh(1, 1, 0, LAST_FIRST)
-        dh(1, 1, 1, LAST_FIRST)
+        dh(1, 1, 0)
+        dh(1, 1, 1)
         project(0, 1)
         dkv(0, 6)
         dq(0, 2)
         weave_z(1, 1)
         row_sum(0, 2)
         quantize("t", 1, 1)
-        flip_z(1, 0, LAST_FIRST)
-        flip_z(1, 1, LAST_FIRST)
+        flip_z(1, 0)
+        flip_z(1, 1)
         project(0, 2)
         quantize("z", 1, 0)
         quantize("z", 1, 1)
         dkv(0, 7)
         dq(0, 3)
         dkv(1, 0, on_vector)
-        flip_k(1, 0, LAST_FIRST)
-        flip_k(1, 1, LAST_FIRST)
+        flip_k(1, 0)
+        flip_k(1, 1)
         row_sum(0, 3)
         quantize("k", 1, 0, 0)
         project(0, 3)
         quantize("k", 1, 0, 1)
-        flip_k(1, 2, LAST_FIRST)
-        flip_k(1, 3, LAST_FIRST)
+        flip_k(1, 2)
+        flip_k(1, 3)
         quantize("k", 1, 1, 0)
         quantize("k", 1, 1, 1)
 

import math
from contextlib import ExitStack

import concourse.mybir as mybir
from concourse.masks import make_identity

B, N, C, E = 2, 512, 1024, 1024
FLOPS = 2 * B * N * C * E + 2 * B * N * E * E + 2 * B * N * E * E
BYTES = 2 * (B * N * E + B * E * E + E * C + B * N * C) + 4 * B * N + 4 * (B * N * E + B * E * E)

F32 = mybir.dt.float32
BF16 = mybir.dt.bfloat16
U32 = mybir.dt.uint32
U8 = mybir.dt.uint8
E4M3 = mybir.dt.float8_e4m3fn_x4
E5M2 = mybir.dt.float8_e5m2_x4
ALU = mybir.AluOpType
ACT = mybir.ActivationFunctionType

P = 128
BANK = 512
PSUM_BANKS = 8

RAW_BUFS = 10
STAGE_BUFS = 7
DZ_BUFS = 4
DKV_BUFS = 7
SCALED_BUFS = 3
DQ_OUT_BUFS = 4


def tile_essattn_pb_v_kernel(tc, q_feat, kv, v, w_proj, b_proj, rnorm, grad_out, out_0, out_1):
    nc = tc.nc
    with ExitStack() as ctx:
        keep = ctx.enter_context(tc.tile_pool(name="keep", bufs=1))
        flow = ctx.enter_context(tc.tile_pool(name="flow", bufs=2))
        psum = ctx.enter_context(tc.psum_pool(name="psum", bufs=1))
        ctx.enter_context(tc.manual_schedule())

        ident = keep.tile([P, P], F32, name="ident")
        make_identity(nc, ident[:])
        rn = keep.tile([P, B, 4], F32, name="rn")
        neg_rn2 = keep.tile([P, B, 4], F32, name="neg_rn2")

        raw, q_sb, q2, staged, codes, scales, dz, scaled, coef, dq_out = {}, {}, {}, {}, {}, {}, {}, {}, {}, {}
        bank_order = list(range(PSUM_BANKS))

        def bank_pair():
            pair = bank_order[0:2]
            bank_order.extend(pair)
            bank_order.remove(pair[0])
            bank_order.remove(pair[1])
            return [psum.tile([P, BANK], F32, name="bank%d" % k, tag="bank%d" % k) for k in pair]

        def load_rows(key, src):
            raw[key] = flow.tile([P, 2, C], BF16, name="raw", tag="raw", bufs=RAW_BUFS)
            nc.sync.dma_start(out=raw[key][:], in_=src)

        def load_g(b, jp):
            load_rows(("g", b, jp), grad_out[b].rearrange("(p jp a) c -> jp p a c", jp=2, a=2)[jp])

        def load_w(h, uz):
            load_rows(("w", h, uz), w_proj.rearrange("(h p uz a) c -> h uz p a c", h=2, uz=2, a=2)[h, uz])

        def load_k(b, kt):
            load_rows(("k", b, kt), kv[b].rearrange("(kt a p) c -> kt p a c", a=2, p=P)[kt])

        def load_q(b):
            q_sb[b] = keep.tile([P, 4, E], BF16, name="q%d" % b)
            nc.sync.dma_start(out=q_sb[b][:], in_=q_feat[b].rearrange("(p j) e -> p j e", j=4))

        def stage(unit):
            if unit not in staged:
                staged[unit] = flow.tile([P, 4 * BANK], BF16, name="stage", tag="stage", bufs=STAGE_BUFS, align_bytes=64)
            return staged[unit]

        def flip(blocks, units, parts, layout):
            banks = bank_pair()
            for n in range(2):
                for m in range(4):
                    nc.tensor.transpose(banks[n][:, P * m : P * (m + 1)], blocks[n][m], ident[:])
            for n in range(2):
                pairs = stage(units[n])[:].bitcast(F32)[:, BANK * parts[n] : BANK * (parts[n] + 1)]
                nc.scalar.copy(
                    out=pairs.rearrange("p (%s) -> p %s" % (layout, layout), a=2, u=2),
                    in_=banks[n][:].rearrange("p (a u r) -> p %s" % layout, a=2, u=2),
                )

        def raw_blocks(key):
            pairs = raw[key][:].bitcast(F32)
            return [[pairs[:, a, 256 * g + u : 256 * (g + 1) : 2] for a in range(2) for u in range(2)] for g in range(2)]

        def flip_g(b, jp):
            flip(raw_blocks(("g", b, jp)), [("g", b, jp)] * 2, [0, 1], "a r u")

        def flip_w(h, uz):
            flip(raw_blocks(("w", h, uz)), [("w", h, 0), ("w", h, 1)], [uz, uz], "r a u")

        def flip_k(b, kt):
            flip(raw_blocks(("k", b, kt)), [("k", b, kt // 2, 0), ("k", b, kt // 2, 1)], [kt % 2] * 2, "a r u")

        def flip_z(b, h):
            pairs = dz[b, h][:].rearrange("p j c -> p (j c)").bitcast(F32)
            blocks = [[pairs[:, P * (4 * jp + m) : P * (4 * jp + m + 1)] for m in range(4)] for jp in range(2)]
            flip(blocks, [("z", b, h)] * 2, [0, 1], "a r u")

        def weave(unit, slots):
            nc.vector.tensor_copy(
                out=stage(unit)[:].rearrange("p (c x j) -> p c j x", x=4, j=4),
                in_=slots.rearrange("p j (c x) -> p c j x", x=4),
            )

        def weave_z(b, h):
            weave(("t", b, h), dz[b, h][:])

        def scale_q(b):
            q2[b] = flow.tile([P, 4, E], BF16, name="q2", tag="q2", bufs=1)
            for j in range(4):
                nc.vector.tensor_scalar(
                    out=q2[b][:, j, :], in0=q_sb[b][:, j, :], scalar1=rn[:, b, j : j + 1], scalar2=None, op0=ALU.mult
                )

        def weave_q(b, half):
            weave(("q", b, half), q2[b][:, :, BANK * half : BANK * (half + 1)])

        def fmt(unit):
            return E4M3 if unit[0] in ("w", "k", "q") else E5M2

        def quantize(*unit):
            label = "_".join(str(x) for x in unit)
            codes[unit] = keep.tile([P, BANK], U32, name="codes_" + label, align_bytes=64)
            scales[unit] = keep.tile([P, BANK], U8, name="scales_" + label, align_bytes=64)
            nc.vector.quantize_mx(out=codes[unit][:].bitcast(fmt(unit)), scales=scales[unit][:], in_=staged[unit][:])

        def mx_pass(bank, still, block, moving, start, stop):
            cols = slice(P * block, P * (block + 1))
            nc.tensor.matmul_mx(
                out=bank[:],
                lhsT=codes[still][:, cols].bitcast(fmt(still)),
                lhsT_scale=scales[still][:, cols],
                rhs=codes[moving][:].bitcast(fmt(moving)),
                rhs_scale=scales[moving][:],
                start=start,
                stop=stop,
            )

        def dh(b, h, jp):
            if jp == 0:
                dz[b, h] = flow.tile([P, 4, BANK], BF16, name="dz", tag="dz", bufs=DZ_BUFS)
            banks = bank_pair()
            for a in range(2):
                for g in range(2):
                    mx_pass(banks[a], ("g", b, jp), 2 * g + a, ("w", h, g), g == 0, g == 1)
            for a in range(2):
                nc.scalar.activation(out=dz[b, h][:, 2 * jp + a, :], in_=banks[a][:], func=ACT.Copy, scale=1.0 / math.sqrt(N))

        def dkv(b, i, copies=(nc.scalar.copy, nc.scalar.copy)):
            res = flow.tile([P, 2, BANK], F32, name="dkv", tag="dkv", bufs=DKV_BUFS)
            banks = bank_pair()
            for h in range(2):
                mx_pass(banks[h], ("q", b, i // 4), i % 4, ("t", b, h), True, True)
            for h in range(2):
                copies[h](
                    out=res[:, h, :].rearrange("p (r uz a) -> p r uz a", uz=2, a=2),
                    in_=banks[h][:].rearrange("p (uz r a) -> p r uz a", uz=2, a=2),
                )
            nc.sync.dma_start(out=out_1[b, P * i : P * (i + 1), :], in_=res[:].rearrange("p h c -> p (h c)"))

        def dq(b, j):
            scaled[b, j] = flow.tile([P, E], F32, name="scaled", tag="scaled", bufs=SCALED_BUFS)
            banks = bank_pair()
            for half in range(2):
                for g in range(2):
                    mx_pass(banks[half], ("z", b, g), j, ("k", b, half, g), g == 0, g == 1)
            for half in range(2):
                nc.scalar.activation(
                    out=scaled[b, j][:, BANK * half : BANK * (half + 1)], in_=banks[half][:], func=ACT.Copy, scale=rn[:, b, j : j + 1]
                )

        def row_sum(b, j):
            coef[b, j] = flow.tile([P, 1], F32, name="coef", tag="coef")
            dq_out[b, j] = flow.tile([P, E], F32, name="dq_out", tag="dq_out", bufs=DQ_OUT_BUFS)
            nc.vector.scalar_tensor_tensor(
                out=dq_out[b, j][:],
                in0=scaled[b, j][:],
                scalar=neg_rn2[:, b, j : j + 1],
                in1=q_sb[b][:, j, :],
                op0=ALU.mult,
                op1=ALU.mult,
                accum_out=coef[b, j][:],
            )

        def project(b, j, pieces=1):
            rows = out_0[b].rearrange("(p j) e -> j p e", j=4)[j]
            for n in range(pieces):
                cols = slice(E * n // pieces, E * (n + 1) // pieces)
                nc.vector.scalar_tensor_tensor(
                    out=dq_out[b, j][:, cols],
                    in0=q_sb[b][:, j, cols],
                    scalar=coef[b, j][:],
                    in1=scaled[b, j][:, cols],
                    op0=ALU.mult,
                    op1=ALU.add,
                )
                nc.sync.dma_start(out=rows[:, cols], in_=dq_out[b, j][:, cols])

        on_vector = (nc.vector.tensor_copy, nc.vector.tensor_copy)
        shared = (nc.scalar.copy, nc.vector.tensor_copy)

        nc.scalar.dma_start(out=rn[:], in_=rnorm.rearrange("b (p j) o -> p b (j o)", j=4))
        load_g(0, 0)
        load_w(0, 0)
        load_w(0, 1)
        load_g(0, 1)
        load_q(0)
        load_w(1, 0)
        load_w(1, 1)
        for kt in range(4):
            load_k(0, kt)
        load_q(1)

        flip_g(0, 0)
        quantize("g", 0, 0)
        flip_w(0, 0)
        flip_w(0, 1)
        quantize("w", 0, 0)
        quantize("w", 0, 1)
        flip_g(0, 1)
        quantize("g", 0, 1)
        load_g(1, 0)
        load_g(1, 1)
        load_k(1, 0)
        load_k(1, 1)
        scale_q(0)
        weave_q(0, 0)
        dh(0, 0, 0)
        dh(0, 0, 1)
        flip_w(1, 0)
        flip_w(1, 1)
        weave_q(0, 1)
        quantize("w", 1, 0)
        quantize("w", 1, 1)
        load_k(1, 2)
        load_k(1, 3)
        weave_z(0, 0)
        quantize("q", 0, 0)
        quantize("q", 0, 1)
        quantize("t", 0, 0)
        flip_k(0, 0)
        flip_k(0, 1)
        dh(0, 1, 0)
        dh(0, 1, 1)
        quantize("k", 0, 0, 0)
        quantize("k", 0, 0, 1)
        scale_q(1)
        flip_z(0, 0)
        flip_z(0, 1)
        weave_z(0, 1)
        quantize("z", 0, 0)
        quantize("t", 0, 1)
        quantize("z", 0, 1)
        flip_k(0, 2)
        flip_k(0, 3)
        weave_q(1, 0)
        nc.vector.scalar_tensor_tensor(out=neg_rn2[:], in0=rn[:], scalar=-1.0, in1=rn[:], op0=ALU.mult, op1=ALU.mult)
        quantize("k", 0, 1, 0)
        quantize("k", 0, 1, 1)

        dkv(0, 0)
        dkv(0, 1)
        flip_g(1, 0)
        flip_g(1, 1)
        weave_q(1, 1)
        quantize("g", 1, 0)
        quantize("g", 1, 1)
        dkv(0, 2)
        dq(0, 0)
        dkv(0, 3, on_vector)
        quantize("q", 1, 0)
        row_sum(0, 0)
        dh(1, 0, 0)
        dh(1, 0, 1)
        quantize("q", 1, 1)
        project(0, 0)
        dkv(0, 4)
        dq(0, 1)
        dkv(0, 5, on_vector)
        weave_z(1, 0)
        row_sum(0, 1)
        quantize("t", 1, 0)
        dh(1, 1, 0)
        dh(1, 1, 1)
        project(0, 1)
        dkv(0, 6)
        dq(0, 2)
        weave_z(1, 1)
        row_sum(0, 2)
        quantize("t", 1, 1)
        flip_z(1, 0)
        flip_z(1, 1)
        project(0, 2)
        quantize("z", 1, 0)
        quantize("z", 1, 1)
        dkv(0, 7)
        dq(0, 3)
        dkv(1, 0, on_vector)
        flip_k(1, 0)
        flip_k(1, 1)
        row_sum(0, 3)
        quantize("k", 1, 0, 0)
        project(0, 3)
        quantize("k", 1, 0, 1)
        flip_k(1, 2)
        flip_k(1, 3)
        quantize("k", 1, 1, 0)
        quantize("k", 1, 1, 1)

        dkv(1, 1)
        dkv(1, 2, on_vector)
        dkv(1, 3, shared)
        dq(1, 0)
        dq(1, 1)
        row_sum(1, 0)
        dkv(1, 4)
        row_sum(1, 1)
        project(1, 0)
        dq(1, 2)
        dkv(1, 5)
        project(1, 1)
        dq(1, 3)
        row_sum(1, 2)
        dkv(1, 6)
        row_sum(1, 3)
        dkv(1, 7)
        project(1, 2)
        project(1, 3, pieces=2)
